import numpy as np
import ml_dtypes

BF16 = ml_dtypes.bfloat16


def bf(x):
    return np.asarray(x, np.float32).astype(BF16)


def f32(x):
    return np.asarray(x, np.float32)


def f64(x):
    return np.asarray(x).astype(np.float64)


def striped(idx):
    return np.tile(idx.reshape(-1, 16).T, (8, 1))


C, S, N = 128, 1024, 512


def sigmoid(v):
    return 1.0 / (1.0 + np.exp(-v))


def setup_inputs():
    return {"base": f32(np.random.standard_normal((C, S))), "emb": f32(np.random.standard_normal((C, N))), "ctx": f32(np.abs(np.random.standard_normal((C, N)))), "gate": f32(np.random.random((C, 1))), "offs": striped(np.random.permutation(S)[:N])}


def reference(base, emb, ctx, gate, offs):
    idx = offs[:16].T.reshape(-1)
    s = sigmoid(f64(gate))
    res = f64(base).copy()
    res[:, idx] = s * f64(emb) + (1.0 - s) * f64(ctx)
    return res

@@ -1,0 +1,39 @@
+import concourse.mybir as mybir
+
+F32 = mybir.dt.float32
+U16 = mybir.dt.uint16
+ADD = mybir.AluOpType.add
+SIGMOID = mybir.ActivationFunctionType.Sigmoid
+COPY = mybir.ActivationFunctionType.Copy
+
+C = 128
+S = 1024
+N = 512
+
+
+def tile_dynamickge_kernel(tc, base, emb, ctx, gate, offs, out):
+    nc = tc.nc
+    with tc.tile_pool(name="held", bufs=1) as held:
+        offsets = held.tile([C, N // 16], U16, name="offsets")
+        gate_in = held.tile([C, 1], F32, name="gate_in")
+        own = held.tile([C, N], F32, name="own")
+        context = held.tile([C, N], F32, name="context")
+        table = held.tile([C, S], F32, name="table")
+        nc.sync.dma_start(offsets[:], offs)
+        nc.sync.dma_start(gate_in[:], gate)
+        nc.sync.dma_start(own[:], emb)
+        nc.sync.dma_start(context[:], ctx)
+        nc.sync.dma_start(table[:], base)
+
+        share_context = held.tile([C, 1], F32, name="share_context")
+        share_own = held.tile([C, 1], F32, name="share_own")
+        nc.scalar.activation(share_context[:], gate_in[:], SIGMOID, scale=-1.0)
+        nc.scalar.activation(share_own[:], gate_in[:], SIGMOID)
+
+        gated_context = held.tile([C, N], F32, name="gated_context")
+        gated_own = held.tile([C, N], F32, name="gated_own")
+        nc.vector.tensor_scalar_mul(gated_context[:], context[:], share_context[:])
+        nc.scalar.activation(gated_own[:], own[:], COPY, scale=share_own[:])
+
+        nc.vector.tensor_tensor(table[:].indirect(offsets[:]), gated_own[:], gated_context[:], ADD)
+        nc.sync.dma_start(out, table[:])

@@ -19,11 +19,13 @@ def tile_dynamickge_kernel(tc, base, emb, ctx, gate, offs, out):
         own = held.tile([C, N], F32, name="own")
         context = held.tile([C, N], F32, name="context")
         table = held.tile([C, S], F32, name="table")
+        HALF = S // 2
         nc.sync.dma_start(offsets[:], offs)
-        nc.sync.dma_start(gate_in[:], gate)
+        nc.scalar.dma_start(gate_in[:], gate)
         nc.sync.dma_start(own[:], emb)
-        nc.sync.dma_start(context[:], ctx)
-        nc.sync.dma_start(table[:], base)
+        nc.scalar.dma_start(context[:], ctx)
+        nc.sync.dma_start(table[:, :HALF], base[:, :HALF])
+        nc.scalar.dma_start(table[:, HALF:], base[:, HALF:])
 
         share_context = held.tile([C, 1], F32, name="share_context")
         share_own = held.tile([C, 1], F32, name="share_own")

@@ -19,13 +19,11 @@ def tile_dynamickge_kernel(tc, base, emb, ctx, gate, offs, out):
         own = held.tile([C, N], F32, name="own")
         context = held.tile([C, N], F32, name="context")
         table = held.tile([C, S], F32, name="table")
-        HALF = S // 2
         nc.sync.dma_start(offsets[:], offs)
-        nc.scalar.dma_start(gate_in[:], gate)
+        nc.sync.dma_start(gate_in[:], gate)
         nc.sync.dma_start(own[:], emb)
-        nc.scalar.dma_start(context[:], ctx)
-        nc.sync.dma_start(table[:, :HALF], base[:, :HALF])
-        nc.scalar.dma_start(table[:, HALF:], base[:, HALF:])
+        nc.sync.dma_start(context[:], ctx)
+        nc.sync.dma_start(table[:], base)
 
         share_context = held.tile([C, 1], F32, name="share_context")
         share_own = held.tile([C, 1], F32, name="share_own")
@@ -38,4 +36,6 @@ def tile_dynamickge_kernel(tc, base, emb, ctx, gate, offs, out):
         nc.scalar.activation(gated_own[:], own[:], COPY, scale=share_own[:])
 
         nc.vector.tensor_tensor(table[:].indirect(offsets[:]), gated_own[:], gated_context[:], ADD)
-        nc.sync.dma_start(out, table[:])
+        HALF = S // 2
+        nc.sync.dma_start(out[:, :HALF], table[:, :HALF])
+        nc.scalar.dma_start(out[:, HALF:], table[:, HALF:])

@@ -1,10 +1,12 @@
+import math
+
 import concourse.mybir as mybir
 
 F32 = mybir.dt.float32
 U16 = mybir.dt.uint16
 ADD = mybir.AluOpType.add
-SIGMOID = mybir.ActivationFunctionType.Sigmoid
-COPY = mybir.ActivationFunctionType.Copy
+MULT = mybir.AluOpType.mult
+POW = mybir.AluOpType.pow
 
 C = 128
 S = 1024
@@ -25,17 +27,20 @@ def tile_dynamickge_kernel(tc, base, emb, ctx, gate, offs, out):
         nc.sync.dma_start(context[:], ctx)
         nc.sync.dma_start(table[:], base)
 
-        share_context = held.tile([C, 1], F32, name="share_context")
+        inverse_e = held.tile([C, 1], F32, name="inverse_e")
+        decay = held.tile([C, 1], F32, name="decay")
+        nc.gpsimd.memset(inverse_e[:], math.exp(-1.0))
+        nc.gpsimd.tensor_tensor(decay[:], inverse_e[:], gate_in[:], POW)
         share_own = held.tile([C, 1], F32, name="share_own")
-        nc.scalar.activation(share_context[:], gate_in[:], SIGMOID, scale=-1.0)
-        nc.scalar.activation(share_own[:], gate_in[:], SIGMOID)
+        share_context = held.tile([C, 1], F32, name="share_context")
+        nc.vector.tensor_scalar_add(decay[:], decay[:], 1.0)
+        nc.vector.reciprocal(share_own[:], decay[:])
+        nc.vector.tensor_scalar(share_context[:], share_own[:], -1.0, 1.0, MULT, ADD)
 
-        gated_context = held.tile([C, N], F32, name="gated_context")
         gated_own = held.tile([C, N], F32, name="gated_own")
+        gated_context = held.tile([C, N], F32, name="gated_context")
+        nc.vector.tensor_scalar_mul(gated_own[:], own[:], share_own[:])
         nc.vector.tensor_scalar_mul(gated_context[:], context[:], share_context[:])
-        nc.scalar.activation(gated_own[:], own[:], COPY, scale=share_own[:])
 
         nc.vector.tensor_tensor(table[:].indirect(offsets[:]), gated_own[:], gated_context[:], ADD)
-        HALF = S // 2
-        nc.sync.dma_start(out[:, :HALF], table[:, :HALF])
-        nc.scalar.dma_start(out[:, HALF:], table[:, HALF:])
+        nc.sync.dma_start(out, table[:])

@@ -1,12 +1,9 @@
-import math
-
 import concourse.mybir as mybir
 
 F32 = mybir.dt.float32
 U16 = mybir.dt.uint16
 ADD = mybir.AluOpType.add
-MULT = mybir.AluOpType.mult
-POW = mybir.AluOpType.pow
+SIGMOID = mybir.ActivationFunctionType.Sigmoid
 
 C = 128
 S = 1024
@@ -27,15 +24,10 @@ def tile_dynamickge_kernel(tc, base, emb, ctx, gate, offs, out):
         nc.sync.dma_start(context[:], ctx)
         nc.sync.dma_start(table[:], base)
 
-        inverse_e = held.tile([C, 1], F32, name="inverse_e")
-        decay = held.tile([C, 1], F32, name="decay")
-        nc.gpsimd.memset(inverse_e[:], math.exp(-1.0))
-        nc.gpsimd.tensor_tensor(decay[:], inverse_e[:], gate_in[:], POW)
         share_own = held.tile([C, 1], F32, name="share_own")
         share_context = held.tile([C, 1], F32, name="share_context")
-        nc.vector.tensor_scalar_add(decay[:], decay[:], 1.0)
-        nc.vector.reciprocal(share_own[:], decay[:])
-        nc.vector.tensor_scalar(share_context[:], share_own[:], -1.0, 1.0, MULT, ADD)
+        nc.scalar.activation(share_own[:], gate_in[:], SIGMOID)
+        nc.scalar.activation(share_context[:], gate_in[:], SIGMOID, scale=-1.0)
 
         gated_own = held.tile([C, N], F32, name="gated_own")
         gated_context = held.tile([C, N], F32, name="gated_context")

@@ -15,9 +15,9 @@ def tile_dynamickge_kernel(tc, base, emb, ctx, gate, offs, out):
     with tc.tile_pool(name="held", bufs=1) as held:
         offsets = held.tile([C, N // 16], U16, name="offsets")
         gate_in = held.tile([C, 1], F32, name="gate_in")
-        own = held.tile([C, N], F32, name="own")
-        context = held.tile([C, N], F32, name="context")
-        table = held.tile([C, S], F32, name="table")
+        own = held.tile([C, N], F32, name="own", align_bytes=256)
+        context = held.tile([C, N], F32, name="context", align_bytes=256)
+        table = held.tile([C, S], F32, name="table", align_bytes=256)
         nc.sync.dma_start(offsets[:], offs)
         nc.sync.dma_start(gate_in[:], gate)
         nc.sync.dma_start(own[:], emb)

@@ -15,9 +15,9 @@ def tile_dynamickge_kernel(tc, base, emb, ctx, gate, offs, out):
     with tc.tile_pool(name="held", bufs=1) as held:
         offsets = held.tile([C, N // 16], U16, name="offsets")
         gate_in = held.tile([C, 1], F32, name="gate_in")
-        own = held.tile([C, N], F32, name="own", align_bytes=256)
-        context = held.tile([C, N], F32, name="context", align_bytes=256)
-        table = held.tile([C, S], F32, name="table", align_bytes=256)
+        own = held.tile([C, N], F32, name="own", align_bytes=4 * N)
+        context = held.tile([C, N], F32, name="context", align_bytes=4 * N)
+        table = held.tile([C, S], F32, name="table", align_bytes=4 * S)
         nc.sync.dma_start(offsets[:], offs)
         nc.sync.dma_start(gate_in[:], gate)
         nc.sync.dma_start(own[:], emb)

import concourse.mybir as mybir

F32 = mybir.dt.float32
U16 = mybir.dt.uint16
ADD = mybir.AluOpType.add
SIGMOID = mybir.ActivationFunctionType.Sigmoid

C = 128
S = 1024
N = 512


def tile_dynamickge_kernel(tc, base, emb, ctx, gate, offs, out):
    nc = tc.nc
    with tc.tile_pool(name="held", bufs=1) as held:
        offsets = held.tile([C, N // 16], U16, name="offsets")
        gate_in = held.tile([C, 1], F32, name="gate_in")
        own = held.tile([C, N], F32, name="own", align_bytes=4 * N)
        context = held.tile([C, N], F32, name="context", align_bytes=4 * N)
        table = held.tile([C, S], F32, name="table", align_bytes=4 * S)
        nc.sync.dma_start(offsets[:], offs)
        nc.sync.dma_start(gate_in[:], gate)
        nc.sync.dma_start(own[:], emb)
        nc.sync.dma_start(context[:], ctx)
        nc.sync.dma_start(table[:], base)

        share_own = held.tile([C, 1], F32, name="share_own")
        share_context = held.tile([C, 1], F32, name="share_context")
        nc.scalar.activation(share_own[:], gate_in[:], SIGMOID)
        nc.scalar.activation(share_context[:], gate_in[:], SIGMOID, scale=-1.0)

        gated_own = held.tile([C, N], F32, name="gated_own")
        gated_context = held.tile([C, N], F32, name="gated_context")
        nc.vector.tensor_scalar_mul(gated_own[:], own[:], share_own[:])
        nc.vector.tensor_scalar_mul(gated_context[:], context[:], share_context[:])

        nc.vector.tensor_tensor(table[:].indirect(offsets[:]), gated_own[:], gated_context[:], ADD)
        nc.sync.dma_start(out, table[:])
